import numpy as np
import ml_dtypes


def mxq(x, axis, fmt="e4m3"):
    dtype, down = {"e4m3": (ml_dtypes.float8_e4m3fn, 7), "e5m2": (ml_dtypes.float8_e5m2, 14)}[fmt]
    v = np.moveaxis(np.asarray(x, np.float32).astype(ml_dtypes.bfloat16).astype(np.float64), axis, -1)
    blocks = v.reshape(v.shape[:-1] + (-1, 32))
    amax = np.abs(blocks).max(-1, keepdims=True)
    byte = np.maximum(np.where(amax > 0, np.frexp(amax)[1] - 1 + 127, 0) - down, 1)
    scale = np.exp2(byte - 127.0)
    codes = (blocks / scale).astype(np.float32).astype(dtype).astype(np.float64)
    return np.moveaxis((codes * scale).reshape(v.shape), -1, axis)


WIDE = False


def mx_kscale(k):
    if not WIDE:
        return np.ones(k)
    levels = np.array([10, -10, 5, -5, 0])
    if k % 512:
        return np.exp2(np.random.permutation(np.resize(levels, k // 32))).repeat(32)
    a = np.empty((k // 512, 16))
    for p in range(k // 512):
        a[p, :8] = np.random.permutation(np.resize(levels, 8))
        for g in range(8):
            far = levels[np.abs(levels - a[p, g]) >= 10]
            a[p, g + 8] = far[np.random.randint(len(far))]
    return np.exp2(a.ravel()).repeat(32)


BF16 = ml_dtypes.bfloat16


def bf(x):
    return np.asarray(x, np.float32).astype(BF16)


def f64(x):
    return np.asarray(x).astype(np.float64)


B, S, HID, NH, DH = 4, 1024, 1024, 4, 64
DQ = NH * DH


def setup_inputs():
    s = mx_kscale(HID)

    def w():
        return bf(np.random.standard_normal((HID, DQ)) / np.sqrt(HID) / s[:, None])

    def b():
        return bf(np.random.standard_normal(DQ) * 0.3)

    return {"x": bf(np.random.standard_normal((B, S, HID)) * s),
            "reasoning_mask": bf(np.random.uniform(size=(B, S, 1, 1))),
            "Wq": w(), "bq": b(), "Wk": w(), "bk": b(),
            "Wqr": w(), "bqr": b(), "Wkr": w(), "bkr": b()}


def reference(x, reasoning_mask, Wq, bq, Wk, bk, Wqr, bqr, Wkr, bkr):
    xq = mxq(f64(x), 2, "e4m3")
    g = f64(reasoning_mask)

    def proj(W, b):
        return ((xq @ mxq(f64(W), 0, "e4m3")) + f64(b)).reshape(B, S, NH, DH)

    q = proj(Wq, bq)
    k = proj(Wk, bk)
    q_r = proj(Wqr, bqr)
    k_r = proj(Wkr, bkr)
    q = q * (1.0 - g) + q_r * g
    k = k * (1.0 - g) + k_r * g
    return q, k

@@ -1,0 +1,293 @@
+from contextlib import ExitStack
+
+import concourse.mybir as mybir
+from concourse.masks import make_identity
+
+F32 = mybir.dt.float32
+BF16 = mybir.dt.bfloat16
+U32 = mybir.dt.uint32
+U8 = mybir.dt.uint8
+FP8X4 = mybir.dt.float8_e4m3fn_x4
+ALU = mybir.AluOpType
+ACT = mybir.ActivationFunctionType
+
+P = 128
+TOKENS = 4 * 1024
+HID = 1024
+FEAT = 256
+PACK = 4
+K_PASS = P * PACK
+PASSES = HID // K_PASS
+BANK = 2 * FEAT
+WORDS = HID // 2
+TILES = TOKENS // P
+GROUP_TILES = 4
+ROUND_TILES = 2
+ROUNDS = TILES // ROUND_TILES
+LAST = ROUNDS - 1
+TOKEN_LEAD = 2
+PSUM_BANKS = 8
+ACC_BANKS = PSUM_BANKS - ROUND_TILES
+RESULT_BUFS = 6
+PLAIN, REASONING = 0, 1
+
+FLOPS = 2 * TOKENS * HID * 4 * FEAT
+
+
+def tile_reasoningmultiheadattention_pa_t_kernel(
+    tc, x, reasoning_mask, Wq, bq, Wk, bk, Wqr, bqr, Wkr, bkr, out_0, out_1
+):
+    nc = tc.nc
+    weights = (Wq, Wk, Wqr, Wkr)
+    biases = (bq, bk, bqr, bkr)
+
+    x_groups = x.rearrange("b s h -> (b s) h").rearrange(
+        "(a p v) h -> a p v h", p=P, v=GROUP_TILES
+    )
+    gate_tiles = reasoning_mask.rearrange("b s o i -> (b s o i)").rearrange(
+        "(a p v) -> p a v", p=P, v=GROUP_TILES
+    )
+    out_groups = [
+        o.rearrange("b s n d -> (b s) (n d)").rearrange("(a p v) f -> a p v f", p=P, v=GROUP_TILES)
+        for o in (out_0, out_1)
+    ]
+
+    with ExitStack() as ctx:
+        keep = ctx.enter_context(tc.tile_pool(name="keep", bufs=1))
+        x_pool = ctx.enter_context(tc.tile_pool(name="x_pool", bufs=ROUNDS))
+        mx_pool = ctx.enter_context(tc.tile_pool(name="mx_pool", bufs=TOKEN_LEAD + 2))
+        blend_pool = ctx.enter_context(tc.tile_pool(name="blend_pool", bufs=3))
+        xt_pool = ctx.enter_context(tc.psum_pool(name="xt_pool", bufs=ROUND_TILES))
+        acc_pool = ctx.enter_context(tc.psum_pool(name="acc_pool", bufs=ACC_BANKS))
+        ctx.enter_context(tc.manual_schedule())
+
+        bias_rows = keep.tile([P, 2, BANK], BF16)
+        nc.vector.memset(bias_rows[:], 0.0)
+        ones = keep.tile([P, P], BF16)
+        nc.vector.memset(ones[:], 1.0)
+        ident = keep.tile([P, P], F32)
+        make_identity(nc, ident[:])
+
+        x_sb = {}
+
+        def load_tokens(r):
+            a, v = divmod(r * ROUND_TILES, GROUP_TILES)
+            x_round = x_pool.tile([P, ROUND_TILES, HID], BF16)
+            nc.sync.dma_start(out=x_round[:], in_=x_groups[a, :, v : v + ROUND_TILES, :])
+            x_sb[r] = x_round
+
+        w_raw = {}
+
+        def load_weights(bank):
+            for side in range(2):
+                raw = keep.tile([P, PASSES * PACK, FEAT], BF16, name="w_raw%d%d" % (bank, side))
+                nc.sync.dma_start(
+                    out=raw[:].rearrange("p (c t) n -> p c t n", t=PACK),
+                    in_=weights[2 * bank + side].rearrange("(c p t) n -> p c t n", p=P, t=PACK),
+                )
+                w_raw[(bank, side)] = raw
+
+        load_tokens(0)
+        load_weights(PLAIN)
+        for bank in (PLAIN, REASONING):
+            for side in range(2):
+                nc.scalar.dma_start(
+                    out=bias_rows[0:1, bank, side * FEAT : (side + 1) * FEAT],
+                    in_=biases[2 * bank + side].unsqueeze(0),
+                )
+        gate_bf = keep.tile([P, TILES], BF16)
+        nc.scalar.dma_start(
+            out=gate_bf[:].rearrange("p (a v) -> p a v", v=GROUP_TILES), in_=gate_tiles
+        )
+        load_tokens(1)
+        load_weights(REASONING)
+        for r in range(2, ROUNDS):
+            load_tokens(r)
+
+        grouped_of = {}
+        codes_of = {}
+        scales_of = {}
+
+        def transpose_tokens(r):
+            grouped = mx_pool.tile([P, ROUND_TILES * HID], BF16, align_bytes=64)
+            grouped_words = grouped[:].bitcast(F32)
+            x_words = x_sb[r][:].rearrange("p t h -> p (t h)").bitcast(F32)
+            for t in range(ROUND_TILES):
+                xt = xt_pool.tile([P, WORDS // P, P], F32)
+                for j in range(WORDS // P):
+                    c, u = divmod(j, 2)
+                    first = t * WORDS + c * 2 * P + u
+                    nc.tensor.transpose(
+                        out=xt[:, j, :],
+                        in_=x_words[:, first : first + 2 * P - u : 2],
+                        identity=ident[:],
+                    )
+                nc.scalar.copy(
+                    out=grouped_words[:, t * WORDS : (t + 1) * WORDS].rearrange(
+                        "p (c m u) -> p c m u", c=PASSES, u=2
+                    ),
+                    in_=xt[:].rearrange("p (c u) m -> p c m u", u=2),
+                )
+            grouped_of[r] = grouped
+
+        def quantise_tokens(r):
+            x_codes = mx_pool.tile([P, ROUND_TILES * PASSES * P], U32, align_bytes=64)
+            x_scales = mx_pool.tile([P, ROUND_TILES * PASSES * P], U8, align_bytes=64)
+            nc.vector.quantize_mx(
+                out=x_codes[:].bitcast(FP8X4), scales=x_scales[:], in_=grouped_of[r][:]
+            )
+            codes_of[r] = x_codes
+            scales_of[r] = x_scales
+
+        w_grouped = keep.tile([P, PASSES, 2, BANK, PACK], BF16, align_bytes=64)
+        w_codes = keep.tile([P, PASSES, 2, BANK], U32, align_bytes=64)
+        w_scales = keep.tile([P, PASSES, 2, BANK], U8, align_bytes=64)
+
+        def regroup_weights(bank):
+            for side in range(2):
+                for c in range(PASSES):
+                    rows = w_raw[(bank, side)][:, c * PACK : (c + 1) * PACK, :].rearrange(
+                        "p t (b i) -> p b t i", i=4
+                    )
+                    words = w_grouped[:, c, bank, side * FEAT : (side + 1) * FEAT, :].rearrange(
+                        "p (b i) t -> p b t i", i=4
+                    )
+                    if bank == REASONING and c == 1:
+                        nc.scalar.copy(out=words, in_=rows)
+                    else:
+                        nc.vector.tensor_copy(out=words, in_=rows)
+
+        def quantise_weights(bank):
+            for c in range(PASSES):
+                nc.vector.quantize_mx(
+                    out=w_codes[:, c, bank, :].bitcast(FP8X4),
+                    scales=w_scales[:, c, bank, :],
+                    in_=w_grouped[:, c, bank, :, :].rearrange("p n t -> p (n t)"),
+                )
+
+        def project(r, t, bank):
+            acc = acc_pool.tile([P, BANK], F32)
+            for c in range(PASSES):
+                cols = slice((t * PASSES + c) * P, (t * PASSES + c + 1) * P)
+                nc.tensor.matmul_mx(
+                    out=acc[:],
+                    lhsT=codes_of[r][:, cols].bitcast(FP8X4),
+                    lhsT_scale=scales_of[r][:, cols],
+                    rhs=w_codes[:, c, bank, :].bitcast(FP8X4),
+                    rhs_scale=w_scales[:, c, bank, :],
+                    start=(c == 0),
+                    stop=(c == PASSES - 1),
+                )
+            return acc[:].rearrange("p (s f) -> p s f", s=2)
+
+        bias_plain = keep.tile([P, 2, FEAT], F32)
+        bias_delta = keep.tile([P, 2, FEAT], F32)
+        gate = keep.tile([P, TILES], F32)
+        one_minus_gate = keep.tile([P, TILES], F32)
+
+        def plain_half(r, bias_of_tile):
+            partials = []
+            for t in range(ROUND_TILES):
+                i = r * ROUND_TILES + t
+                partial = blend_pool.tile([P, 2, FEAT], F32)
+                nc.vector.scalar_tensor_tensor(
+                    out=partial[:],
+                    in0=project(r, t, PLAIN),
+                    scalar=one_minus_gate[:, i : i + 1],
+                    in1=bias_of_tile[t],
+                    op0=ALU.mult,
+                    op1=ALU.add,
+                )
+                partials.append(partial)
+            return partials
+
+        round_shape = [P, 2, ROUND_TILES, FEAT]
+
+        def reasoning_half(r, partials):
+            blended = blend_pool.tile(round_shape, F32)
+            for t in range(ROUND_TILES):
+                i = r * ROUND_TILES + t
+                nc.vector.scalar_tensor_tensor(
+                    out=blended[:, :, t, :],
+                    in0=project(r, t, REASONING),
+                    scalar=gate[:, i : i + 1],
+                    in1=partials[t][:],
+                    op0=ALU.mult,
+                    op1=ALU.add,
+                )
+            return blended
+
+        def scale_delta(r):
+            scaled_delta = blend_pool.tile(round_shape, F32)
+            for t in range(ROUND_TILES):
+                i = r * ROUND_TILES + t
+                nc.scalar.activation(
+                    out=scaled_delta[:, :, t, :],
+                    in_=bias_delta[:],
+                    func=ACT.Copy,
+                    scale=gate[:, i : i + 1],
+                )
+            return scaled_delta
+
+        def store(r, result):
+            a, v = divmod(r * ROUND_TILES, GROUP_TILES)
+            for side in range(2):
+                nc.sync.dma_start(
+                    out=out_groups[side][a, :, v : v + ROUND_TILES, :], in_=result[:, side, :, :]
+                )
+
+        transpose_tokens(0)
+        regroup_weights(PLAIN)
+        quantise_tokens(0)
+        quantise_weights(PLAIN)
+
+        spread_plain = acc_pool.tile([P, BANK], F32, tag="acc")
+        spread_reasoning = acc_pool.tile([P, BANK], F32, tag="acc")
+        nc.tensor.matmul(
+            out=spread_plain[:], lhsT=ones[:], rhs=bias_rows[:, PLAIN, :], start=True, stop=True
+        )
+        nc.tensor.matmul(
+            out=spread_reasoning[:],
+            lhsT=ones[:],
+            rhs=bias_rows[:, REASONING, :],
+            start=True,
+            stop=True,
+        )
+        nc.scalar.copy(out=bias_plain[:].rearrange("p s f -> p (s f)"), in_=spread_plain[:])
+        nc.scalar.copy(out=gate[:], in_=gate_bf[:])
+        nc.scalar.activation(
+            out=one_minus_gate[:], in_=gate_bf[:], func=ACT.Copy, bias=1.0, scale=-1.0
+        )
+        nc.vector.tensor_tensor(
+            out=bias_delta[:].rearrange("p s f -> p (s f)"),
+            in0=spread_reasoning[:],
+            in1=bias_plain[:].rearrange("p s f -> p (s f)"),
+            op=ALU.subtract,
+        )
+
+        transpose_tokens(1)
+        regroup_weights(REASONING)
+        quantise_tokens(1)
+        quantise_weights(REASONING)
+
+        last_bias = keep.tile(round_shape, F32)
+        nc.gpsimd.tensor_tensor(
+            out=last_bias[:],
+            in0=scale_delta(LAST)[:],
+            in1=bias_plain[:].unsqueeze(2).to_broadcast(round_shape),
+            op=ALU.add,
+        )
+
+        for r in range(LAST):
+            partials = plain_half(r, [bias_plain[:]] * ROUND_TILES)
+            if r + TOKEN_LEAD < ROUNDS:
+                transpose_tokens(r + TOKEN_LEAD)
+            scaled_delta = scale_delta(r)
+            blended = reasoning_half(r, partials)
+            if r + TOKEN_LEAD < ROUNDS:
+                quantise_tokens(r + TOKEN_LEAD)
+            result = blend_pool.tile(round_shape, F32, bufs=RESULT_BUFS)
+            nc.gpsimd.tensor_tensor(out=result[:], in0=blended[:], in1=scaled_delta[:], op=ALU.add)
+            store(r, result)
+        partials = plain_half(LAST, [last_bias[:, :, t, :] for t in range(ROUND_TILES)])
+        store(LAST, reasoning_half(LAST, partials))

@@ -29,6 +29,7 @@ TOKEN_LEAD = 2
 PSUM_BANKS = 8
 ACC_BANKS = PSUM_BANKS - ROUND_TILES
 RESULT_BUFS = 6
+MX_ALIGN = 256
 PLAIN, REASONING = 0, 1
 
 FLOPS = 2 * TOKENS * HID * 4 * FEAT
@@ -131,8 +132,8 @@ def tile_reasoningmultiheadattention_pa_t_kernel(
             grouped_of[r] = grouped
 
         def quantise_tokens(r):
-            x_codes = mx_pool.tile([P, ROUND_TILES * PASSES * P], U32, align_bytes=64)
-            x_scales = mx_pool.tile([P, ROUND_TILES * PASSES * P], U8, align_bytes=64)
+            x_codes = mx_pool.tile([P, ROUND_TILES * PASSES * P], U32, align_bytes=MX_ALIGN)
+            x_scales = mx_pool.tile([P, ROUND_TILES * PASSES * P], U8, align_bytes=MX_ALIGN)
             nc.vector.quantize_mx(
                 out=x_codes[:].bitcast(FP8X4), scales=x_scales[:], in_=grouped_of[r][:]
             )
@@ -140,8 +141,8 @@ def tile_reasoningmultiheadattention_pa_t_kernel(
             scales_of[r] = x_scales
 
         w_grouped = keep.tile([P, PASSES, 2, BANK, PACK], BF16, align_bytes=64)
-        w_codes = keep.tile([P, PASSES, 2, BANK], U32, align_bytes=64)
-        w_scales = keep.tile([P, PASSES, 2, BANK], U8, align_bytes=64)
+        w_codes = keep.tile([P, PASSES, 2, BANK], U32, align_bytes=MX_ALIGN)
+        w_scales = keep.tile([P, PASSES, 2, BANK], U8, align_bytes=MX_ALIGN)
 
         def regroup_weights(bank):
             for side in range(2):

from contextlib import ExitStack

import concourse.mybir as mybir
from concourse.masks import make_identity

F32 = mybir.dt.float32
BF16 = mybir.dt.bfloat16
U32 = mybir.dt.uint32
U8 = mybir.dt.uint8
FP8X4 = mybir.dt.float8_e4m3fn_x4
ALU = mybir.AluOpType
ACT = mybir.ActivationFunctionType

P = 128
TOKENS = 4 * 1024
HID = 1024
FEAT = 256
PACK = 4
K_PASS = P * PACK
PASSES = HID // K_PASS
BANK = 2 * FEAT
WORDS = HID // 2
TILES = TOKENS // P
GROUP_TILES = 4
ROUND_TILES = 2
ROUNDS = TILES // ROUND_TILES
LAST = ROUNDS - 1
TOKEN_LEAD = 2
PSUM_BANKS = 8
ACC_BANKS = PSUM_BANKS - ROUND_TILES
RESULT_BUFS = 6
MX_ALIGN = 256
PLAIN, REASONING = 0, 1

FLOPS = 2 * TOKENS * HID * 4 * FEAT


def tile_reasoningmultiheadattention_pa_t_kernel(
    tc, x, reasoning_mask, Wq, bq, Wk, bk, Wqr, bqr, Wkr, bkr, out_0, out_1
):
    nc = tc.nc
    weights = (Wq, Wk, Wqr, Wkr)
    biases = (bq, bk, bqr, bkr)

    x_groups = x.rearrange("b s h -> (b s) h").rearrange(
        "(a p v) h -> a p v h", p=P, v=GROUP_TILES
    )
    gate_tiles = reasoning_mask.rearrange("b s o i -> (b s o i)").rearrange(
        "(a p v) -> p a v", p=P, v=GROUP_TILES
    )
    out_groups = [
        o.rearrange("b s n d -> (b s) (n d)").rearrange("(a p v) f -> a p v f", p=P, v=GROUP_TILES)
        for o in (out_0, out_1)
    ]

    with ExitStack() as ctx:
        keep = ctx.enter_context(tc.tile_pool(name="keep", bufs=1))
        x_pool = ctx.enter_context(tc.tile_pool(name="x_pool", bufs=ROUNDS))
        mx_pool = ctx.enter_context(tc.tile_pool(name="mx_pool", bufs=TOKEN_LEAD + 2))
        blend_pool = ctx.enter_context(tc.tile_pool(name="blend_pool", bufs=3))
        xt_pool = ctx.enter_context(tc.psum_pool(name="xt_pool", bufs=ROUND_TILES))
        acc_pool = ctx.enter_context(tc.psum_pool(name="acc_pool", bufs=ACC_BANKS))
        ctx.enter_context(tc.manual_schedule())

        bias_rows = keep.tile([P, 2, BANK], BF16)
        nc.vector.memset(bias_rows[:], 0.0)
        ones = keep.tile([P, P], BF16)
        nc.vector.memset(ones[:], 1.0)
        ident = keep.tile([P, P], F32)
        make_identity(nc, ident[:])

        x_sb = {}

        def load_tokens(r):
            a, v = divmod(r * ROUND_TILES, GROUP_TILES)
            x_round = x_pool.tile([P, ROUND_TILES, HID], BF16)
            nc.sync.dma_start(out=x_round[:], in_=x_groups[a, :, v : v + ROUND_TILES, :])
            x_sb[r] = x_round

        w_raw = {}

        def load_weights(bank):
            for side in range(2):
                raw = keep.tile([P, PASSES * PACK, FEAT], BF16, name="w_raw%d%d" % (bank, side))
                nc.sync.dma_start(
                    out=raw[:].rearrange("p (c t) n -> p c t n", t=PACK),
                    in_=weights[2 * bank + side].rearrange("(c p t) n -> p c t n", p=P, t=PACK),
                )
                w_raw[(bank, side)] = raw

        load_tokens(0)
        load_weights(PLAIN)
        for bank in (PLAIN, REASONING):
            for side in range(2):
                nc.scalar.dma_start(
                    out=bias_rows[0:1, bank, side * FEAT : (side + 1) * FEAT],
                    in_=biases[2 * bank + side].unsqueeze(0),
                )
        gate_bf = keep.tile([P, TILES], BF16)
        nc.scalar.dma_start(
            out=gate_bf[:].rearrange("p (a v) -> p a v", v=GROUP_TILES), in_=gate_tiles
        )
        load_tokens(1)
        load_weights(REASONING)
        for r in range(2, ROUNDS):
            load_tokens(r)

        grouped_of = {}
        codes_of = {}
        scales_of = {}

        def transpose_tokens(r):
            grouped = mx_pool.tile([P, ROUND_TILES * HID], BF16, align_bytes=64)
            grouped_words = grouped[:].bitcast(F32)
            x_words = x_sb[r][:].rearrange("p t h -> p (t h)").bitcast(F32)
            for t in range(ROUND_TILES):
                xt = xt_pool.tile([P, WORDS // P, P], F32)
                for j in range(WORDS // P):
                    c, u = divmod(j, 2)
                    first = t * WORDS + c * 2 * P + u
                    nc.tensor.transpose(
                        out=xt[:, j, :],
                        in_=x_words[:, first : first + 2 * P - u : 2],
                        identity=ident[:],
                    )
                nc.scalar.copy(
                    out=grouped_words[:, t * WORDS : (t + 1) * WORDS].rearrange(
                        "p (c m u) -> p c m u", c=PASSES, u=2
                    ),
                    in_=xt[:].rearrange("p (c u) m -> p c m u", u=2),
                )
            grouped_of[r] = grouped

        def quantise_tokens(r):
            x_codes = mx_pool.tile([P, ROUND_TILES * PASSES * P], U32, align_bytes=MX_ALIGN)
            x_scales = mx_pool.tile([P, ROUND_TILES * PASSES * P], U8, align_bytes=MX_ALIGN)
            nc.vector.quantize_mx(
                out=x_codes[:].bitcast(FP8X4), scales=x_scales[:], in_=grouped_of[r][:]
            )
            codes_of[r] = x_codes
            scales_of[r] = x_scales

        w_grouped = keep.tile([P, PASSES, 2, BANK, PACK], BF16, align_bytes=64)
        w_codes = keep.tile([P, PASSES, 2, BANK], U32, align_bytes=MX_ALIGN)
        w_scales = keep.tile([P, PASSES, 2, BANK], U8, align_bytes=MX_ALIGN)

        def regroup_weights(bank):
            for side in range(2):
                for c in range(PASSES):
                    rows = w_raw[(bank, side)][:, c * PACK : (c + 1) * PACK, :].rearrange(
                        "p t (b i) -> p b t i", i=4
                    )
                    words = w_grouped[:, c, bank, side * FEAT : (side + 1) * FEAT, :].rearrange(
                        "p (b i) t -> p b t i", i=4
                    )
                    if bank == REASONING and c == 1:
                        nc.scalar.copy(out=words, in_=rows)
                    else:
                        nc.vector.tensor_copy(out=words, in_=rows)

        def quantise_weights(bank):
            for c in range(PASSES):
                nc.vector.quantize_mx(
                    out=w_codes[:, c, bank, :].bitcast(FP8X4),
                    scales=w_scales[:, c, bank, :],
                    in_=w_grouped[:, c, bank, :, :].rearrange("p n t -> p (n t)"),
                )

        def project(r, t, bank):
            acc = acc_pool.tile([P, BANK], F32)
            for c in range(PASSES):
                cols = slice((t * PASSES + c) * P, (t * PASSES + c + 1) * P)
                nc.tensor.matmul_mx(
                    out=acc[:],
                    lhsT=codes_of[r][:, cols].bitcast(FP8X4),
                    lhsT_scale=scales_of[r][:, cols],
                    rhs=w_codes[:, c, bank, :].bitcast(FP8X4),
                    rhs_scale=w_scales[:, c, bank, :],
                    start=(c == 0),
                    stop=(c == PASSES - 1),
                )
            return acc[:].rearrange("p (s f) -> p s f", s=2)

        bias_plain = keep.tile([P, 2, FEAT], F32)
        bias_delta = keep.tile([P, 2, FEAT], F32)
        gate = keep.tile([P, TILES], F32)
        one_minus_gate = keep.tile([P, TILES], F32)

        def plain_half(r, bias_of_tile):
            partials = []
            for t in range(ROUND_TILES):
                i = r * ROUND_TILES + t
                partial = blend_pool.tile([P, 2, FEAT], F32)
                nc.vector.scalar_tensor_tensor(
                    out=partial[:],
                    in0=project(r, t, PLAIN),
                    scalar=one_minus_gate[:, i : i + 1],
                    in1=bias_of_tile[t],
                    op0=ALU.mult,
                    op1=ALU.add,
                )
                partials.append(partial)
            return partials

        round_shape = [P, 2, ROUND_TILES, FEAT]

        def reasoning_half(r, partials):
            blended = blend_pool.tile(round_shape, F32)
            for t in range(ROUND_TILES):
                i = r * ROUND_TILES + t
                nc.vector.scalar_tensor_tensor(
                    out=blended[:, :, t, :],
                    in0=project(r, t, REASONING),
                    scalar=gate[:, i : i + 1],
                    in1=partials[t][:],
                    op0=ALU.mult,
                    op1=ALU.add,
                )
            return blended

        def scale_delta(r):
            scaled_delta = blend_pool.tile(round_shape, F32)
            for t in range(ROUND_TILES):
                i = r * ROUND_TILES + t
                nc.scalar.activation(
                    out=scaled_delta[:, :, t, :],
                    in_=bias_delta[:],
                    func=ACT.Copy,
                    scale=gate[:, i : i + 1],
                )
            return scaled_delta

        def store(r, result):
            a, v = divmod(r * ROUND_TILES, GROUP_TILES)
            for side in range(2):
                nc.sync.dma_start(
                    out=out_groups[side][a, :, v : v + ROUND_TILES, :], in_=result[:, side, :, :]
                )

        transpose_tokens(0)
        regroup_weights(PLAIN)
        quantise_tokens(0)
        quantise_weights(PLAIN)

        spread_plain = acc_pool.tile([P, BANK], F32, tag="acc")
        spread_reasoning = acc_pool.tile([P, BANK], F32, tag="acc")
        nc.tensor.matmul(
            out=spread_plain[:], lhsT=ones[:], rhs=bias_rows[:, PLAIN, :], start=True, stop=True
        )
        nc.tensor.matmul(
            out=spread_reasoning[:],
            lhsT=ones[:],
            rhs=bias_rows[:, REASONING, :],
            start=True,
            stop=True,
        )
        nc.scalar.copy(out=bias_plain[:].rearrange("p s f -> p (s f)"), in_=spread_plain[:])
        nc.scalar.copy(out=gate[:], in_=gate_bf[:])
        nc.scalar.activation(
            out=one_minus_gate[:], in_=gate_bf[:], func=ACT.Copy, bias=1.0, scale=-1.0
        )
        nc.vector.tensor_tensor(
            out=bias_delta[:].rearrange("p s f -> p (s f)"),
            in0=spread_reasoning[:],
            in1=bias_plain[:].rearrange("p s f -> p (s f)"),
            op=ALU.subtract,
        )

        transpose_tokens(1)
        regroup_weights(REASONING)
        quantise_tokens(1)
        quantise_weights(REASONING)

        last_bias = keep.tile(round_shape, F32)
        nc.gpsimd.tensor_tensor(
            out=last_bias[:],
            in0=scale_delta(LAST)[:],
            in1=bias_plain[:].unsqueeze(2).to_broadcast(round_shape),
            op=ALU.add,
        )

        for r in range(LAST):
            partials = plain_half(r, [bias_plain[:]] * ROUND_TILES)
            if r + TOKEN_LEAD < ROUNDS:
                transpose_tokens(r + TOKEN_LEAD)
            scaled_delta = scale_delta(r)
            blended = reasoning_half(r, partials)
            if r + TOKEN_LEAD < ROUNDS:
                quantise_tokens(r + TOKEN_LEAD)
            result = blend_pool.tile(round_shape, F32, bufs=RESULT_BUFS)
            nc.gpsimd.tensor_tensor(out=result[:], in0=blended[:], in1=scaled_delta[:], op=ALU.add)
            store(r, result)
        partials = plain_half(LAST, [last_bias[:, :, t, :] for t in range(ROUND_TILES)])
        store(LAST, reasoning_half(LAST, partials))
